import numpy as np
import ml_dtypes


def mxq(x, axis, fmt="e4m3"):
    dtype, down = {"e4m3": (ml_dtypes.float8_e4m3fn, 7), "e5m2": (ml_dtypes.float8_e5m2, 14)}[fmt]
    v = np.moveaxis(np.asarray(x, np.float32).astype(ml_dtypes.bfloat16).astype(np.float64), axis, -1)
    blocks = v.reshape(v.shape[:-1] + (-1, 32))
    amax = np.abs(blocks).max(-1, keepdims=True)
    byte = np.maximum(np.where(amax > 0, np.frexp(amax)[1] - 1 + 127, 0) - down, 1)
    scale = np.exp2(byte - 127.0)
    codes = (blocks / scale).astype(np.float32).astype(dtype).astype(np.float64)
    return np.moveaxis((codes * scale).reshape(v.shape), -1, axis)


WIDE = False


def mx_kscale(k):
    if not WIDE:
        return np.ones(k)
    levels = np.array([20, -20, 10, -10, 0])
    a = np.random.permutation(np.resize(levels, k // 512 * 4)).reshape(k // 512, 4)
    idx = np.arange(k)
    return np.exp2(a[idx // 512, idx % 128 // 32])


BF16 = ml_dtypes.bfloat16


def bf(x):
    return np.asarray(x, np.float32).astype(BF16)


def f64(x):
    return np.asarray(x).astype(np.float64)


N, P, D, E, F = 1024, 3, 512, 1024, 1024


def setup_inputs():
    u = mx_kscale(E)
    x = np.random.standard_normal((N, P, D)) + 0.5 * np.random.standard_normal((1, P, D))
    w1a = np.random.standard_normal((D, E)) / np.sqrt(D) / u[None, :]
    w2a = np.random.standard_normal((D, E)) / np.sqrt(D) / u[None, :]
    g = np.random.standard_normal((N, P, E)) * np.exp2(np.random.randint(-12, 1, (N, P, 1))) * 4.0 * u
    return {"x": bf(x), "w1a": bf(w1a), "w2a": bf(w2a), "grad_out": bf(g)}


def reference(x, w1a, w2a, grad_out):
    gq = mxq(f64(grad_out), 2, "e5m2")
    a = gq @ mxq(f64(w2a), 1, "e4m3").T
    b = gq @ mxq(f64(w1a), 1, "e4m3").T
    return a + (b.sum(axis=1, keepdims=True) - b) * 0.5

@@ -1,0 +1,144 @@
+import concourse.mybir as mybir
+from concourse.masks import make_identity
+
+F32 = mybir.dt.float32
+BF16 = mybir.dt.bfloat16
+U32 = mybir.dt.uint32
+U8 = mybir.dt.uint8
+E4M3_X4 = mybir.dt.float8_e4m3fn_x4
+E5M2_X4 = mybir.dt.float8_e5m2_x4
+ADD = mybir.AluOpType.add
+MULT = mybir.AluOpType.mult
+
+ITEMS, HOPS, D_IN, D_OUT = 1024, 3, 512, 1024
+
+P = 128
+PACK = 4
+HALVES = 2
+K_PASS = P * PACK
+PASSES = D_OUT // K_PASS
+BLOCKS = ITEMS // P
+W_CHUNKS = D_IN // P
+BANK = 512
+PSUM_BANKS = 8
+
+FLOPS = 2 * 2 * ITEMS * HOPS * D_OUT * D_IN
+BYTES = 2 * ITEMS * HOPS * D_OUT + 2 * 2 * D_IN * D_OUT + 4 * ITEMS * HOPS * D_IN
+
+
+def transpose_rows(nc, banks, identity, rows):
+    words = rows.bitcast(F32)
+    bank = banks.tile([P, BANK], F32, name="bank", tag="bank")
+    for j in range(PASSES * HALVES):
+        cols = slice(j * P, (j + 1) * P)
+        nc.tensor.transpose(bank[:, cols], words[:, cols], identity[:])
+    return bank
+
+
+def words_side_by_side(bank):
+    return bank[:].rearrange("p (g u c) -> p g c u", g=PASSES, u=HALVES)
+
+
+def as_words(grouped):
+    return grouped[:].bitcast(F32).rearrange("p (g c u) -> p g c u", g=PASSES, u=HALVES)
+
+
+def mx_product(nc, banks, g_codes, g_scales, w_codes, w_scales):
+    bank = banks.tile([P, BANK], F32, name="bank", tag="bank")
+    for g in range(PASSES):
+        items = slice(g * P, (g + 1) * P)
+        features = slice(g * D_IN, (g + 1) * D_IN)
+        nc.tensor.matmul_mx(
+            out=bank[:],
+            lhsT=g_codes[:, items].bitcast(E5M2_X4),
+            lhsT_scale=g_scales[:, items],
+            rhs=w_codes[:, features].bitcast(E4M3_X4),
+            rhs_scale=w_scales[:, features],
+            start=(g == 0),
+            stop=(g == PASSES - 1),
+        )
+    return bank
+
+
+def tile_dogtaitujuanji_pa_kernel(tc, x, w1a, w2a, grad_out, out):
+    nc = tc.nc
+    with (
+        tc.manual_schedule(),
+        tc.tile_pool(name="const", bufs=1) as const,
+        tc.tile_pool(name="w_rows", bufs=2 * W_CHUNKS) as w_rows,
+        tc.tile_pool(name="g_rows", bufs=BLOCKS * HOPS) as g_rows,
+        tc.tile_pool(name="w_keep", bufs=2) as w_keep,
+        tc.tile_pool(name="stage", bufs=3 * HOPS) as stage,
+        tc.psum_pool(name="banks", bufs=PSUM_BANKS) as banks,
+    ):
+        identity = const.tile([P, P], F32)
+        make_identity(nc, identity[:])
+
+        w_raw = []
+        for w in (w1a, w2a):
+            for chunk in range(W_CHUNKS):
+                w_piece = w_rows.tile([P, D_OUT], BF16)
+                nc.sync.dma_start(out=w_piece[:], in_=w[chunk * P : (chunk + 1) * P, :])
+                w_raw.append(w_piece)
+        g_raw = []
+        for block in range(BLOCKS):
+            for hop in range(HOPS):
+                g_piece = g_rows.tile([P, D_OUT], BF16)
+                nc.sync.dma_start(out=g_piece[:], in_=grad_out[block * P : (block + 1) * P, hop, :])
+                g_raw.append(g_piece)
+
+        def quantise_weight(pieces):
+            w_grouped = w_keep.tile([P, PASSES * D_IN * PACK], BF16, align_bytes=64)
+            for chunk in range(W_CHUNKS):
+                bank = transpose_rows(nc, banks, identity, pieces[chunk][:])
+                nc.vector.tensor_copy(
+                    out=as_words(w_grouped)[:, :, chunk * P : (chunk + 1) * P, :],
+                    in_=words_side_by_side(bank),
+                )
+            w_codes = w_keep.tile([P, PASSES * D_IN], U32, align_bytes=64)
+            w_scales = w_keep.tile([P, PASSES * D_IN], U8, align_bytes=64)
+            nc.vector.quantize_mx(out=w_codes[:].bitcast(E4M3_X4), scales=w_scales[:], in_=w_grouped[:])
+            return w_codes, w_scales
+
+        w1_codes, w1_scales = quantise_weight(w_raw[:W_CHUNKS])
+        w2_codes, w2_scales = quantise_weight(w_raw[W_CHUNKS:])
+
+        def quantise_block(block):
+            quantised = []
+            for hop in range(HOPS):
+                bank = transpose_rows(nc, banks, identity, g_raw[block * HOPS + hop][:])
+                g_grouped = stage.tile([P, PASSES * P * PACK], BF16, align_bytes=64)
+                nc.scalar.copy(out=as_words(g_grouped), in_=words_side_by_side(bank))
+                g_codes = stage.tile([P, PASSES * P], U32, align_bytes=64)
+                g_scales = stage.tile([P, PASSES * P], U8, align_bytes=64)
+                nc.vector.quantize_mx(out=g_codes[:].bitcast(E5M2_X4), scales=g_scales[:], in_=g_grouped[:])
+                quantised.append((g_codes, g_scales))
+            return quantised
+
+        def multiply_block(block, quantised):
+            b_of_hop = []
+            for g_codes, g_scales in quantised:
+                b_bank = mx_product(nc, banks, g_codes, g_scales, w1_codes, w1_scales)
+                b_sb = stage.tile([P, D_IN], F32)
+                nc.scalar.copy(out=b_sb[:], in_=b_bank[:])
+                b_of_hop.append(b_sb)
+            pair_for_hop = []
+            for hop in range(HOPS):
+                q, r = [other for other in range(HOPS) if other != hop]
+                pair = stage.tile([P, D_IN], F32)
+                nc.vector.tensor_tensor(out=pair[:], in0=b_of_hop[q][:], in1=b_of_hop[r][:], op=ADD)
+                pair_for_hop.append(pair)
+            for hop in range(HOPS):
+                g_codes, g_scales = quantised[hop]
+                a_bank = mx_product(nc, banks, g_codes, g_scales, w2_codes, w2_scales)
+                result = stage.tile([P, D_IN], F32)
+                nc.vector.scalar_tensor_tensor(
+                    out=result[:], in0=pair_for_hop[hop][:], scalar=0.5, in1=a_bank[:], op0=MULT, op1=ADD
+                )
+                nc.sync.dma_start(out=out[block * P : (block + 1) * P, hop, :], in_=result[:])
+
+        ready = quantise_block(0)
+        for block in range(BLOCKS):
+            following = quantise_block(block + 1) if block + 1 < BLOCKS else None
+            multiply_block(block, ready)
+            ready = following

@@ -126,7 +126,7 @@ def tile_dogtaitujuanji_pa_kernel(tc, x, w1a, w2a, grad_out, out):
             for hop in range(HOPS):
                 q, r = [other for other in range(HOPS) if other != hop]
                 pair = stage.tile([P, D_IN], F32)
-                nc.vector.tensor_tensor(out=pair[:], in0=b_of_hop[q][:], in1=b_of_hop[r][:], op=ADD)
+                nc.gpsimd.tensor_tensor(out=pair[:], in0=b_of_hop[q][:], in1=b_of_hop[r][:], op=ADD)
                 pair_for_hop.append(pair)
             for hop in range(HOPS):
                 g_codes, g_scales = quantised[hop]

@@ -116,17 +116,24 @@ def tile_dogtaitujuanji_pa_kernel(tc, x, w1a, w2a, grad_out, out):
             return quantised
 
         def multiply_block(block, quantised):
-            b_of_hop = []
-            for g_codes, g_scales in quantised:
+            b_bank_of_hop = []
+            b_copy_of_hop = []
+            for hop in range(HOPS):
+                g_codes, g_scales = quantised[hop]
                 b_bank = mx_product(nc, banks, g_codes, g_scales, w1_codes, w1_scales)
-                b_sb = stage.tile([P, D_IN], F32)
-                nc.scalar.copy(out=b_sb[:], in_=b_bank[:])
-                b_of_hop.append(b_sb)
+                b_bank_of_hop.append(b_bank)
+                if hop < HOPS - 1:
+                    b_copy = stage.tile([P, D_IN], F32)
+                    nc.scalar.copy(out=b_copy[:], in_=b_bank[:])
+                    b_copy_of_hop.append(b_copy)
             pair_for_hop = []
             for hop in range(HOPS):
                 q, r = [other for other in range(HOPS) if other != hop]
                 pair = stage.tile([P, D_IN], F32)
-                nc.gpsimd.tensor_tensor(out=pair[:], in0=b_of_hop[q][:], in1=b_of_hop[r][:], op=ADD)
+                if r == HOPS - 1:
+                    nc.vector.tensor_tensor(out=pair[:], in0=b_bank_of_hop[r][:], in1=b_copy_of_hop[q][:], op=ADD)
+                else:
+                    nc.gpsimd.tensor_tensor(out=pair[:], in0=b_copy_of_hop[q][:], in1=b_copy_of_hop[r][:], op=ADD)
                 pair_for_hop.append(pair)
             for hop in range(HOPS):
                 g_codes, g_scales = quantised[hop]

@@ -21,6 +21,9 @@ BLOCKS = ITEMS // P
 W_CHUNKS = D_IN // P
 BANK = 512
 PSUM_BANKS = 8
+WARM_FIRST = 4
+WARM_EVERY = 2
+WARM_EACH = 2
 
 FLOPS = 2 * 2 * ITEMS * HOPS * D_OUT * D_IN
 BYTES = 2 * ITEMS * HOPS * D_OUT + 2 * 2 * D_IN * D_OUT + 4 * ITEMS * HOPS * D_IN
@@ -74,6 +77,23 @@ def tile_dogtaitujuanji_pa_kernel(tc, x, w1a, w2a, grad_out, out):
         identity = const.tile([P, P], F32)
         make_identity(nc, identity[:])
 
+        zeros = const.tile([P, BANK], BF16)
+        nc.vector.memset(zeros[:], 0.0)
+
+        def keep_warm(count):
+            bank = banks.tile([P, BANK], F32, name="bank", tag="bank")
+            for repeat in range(count):
+                nc.tensor.matmul(out=bank[:], lhsT=zeros[:, :P], rhs=zeros[:], start=True, stop=True)
+
+        groups_seen = []
+
+        def keep_warm_after_group():
+            groups_seen.append(1)
+            if len(groups_seen) % WARM_EVERY == 0:
+                keep_warm(WARM_EACH)
+
+        keep_warm(WARM_FIRST)
+
         w_raw = []
         for w in (w1a, w2a):
             for chunk in range(W_CHUNKS):
@@ -91,6 +111,7 @@ def tile_dogtaitujuanji_pa_kernel(tc, x, w1a, w2a, grad_out, out):
             w_grouped = w_keep.tile([P, PASSES * D_IN * PACK], BF16, align_bytes=64)
             for chunk in range(W_CHUNKS):
                 bank = transpose_rows(nc, banks, identity, pieces[chunk][:])
+                keep_warm_after_group()
                 nc.vector.tensor_copy(
                     out=as_words(w_grouped)[:, :, chunk * P : (chunk + 1) * P, :],
                     in_=words_side_by_side(bank),
@@ -107,6 +128,8 @@ def tile_dogtaitujuanji_pa_kernel(tc, x, w1a, w2a, grad_out, out):
             quantised = []
             for hop in range(HOPS):
                 bank = transpose_rows(nc, banks, identity, g_raw[block * HOPS + hop][:])
+                if block < 2:
+                    keep_warm_after_group()
                 g_grouped = stage.tile([P, PASSES * P * PACK], BF16, align_bytes=64)
                 nc.scalar.copy(out=as_words(g_grouped), in_=words_side_by_side(bank))
                 g_codes = stage.tile([P, PASSES * P], U32, align_bytes=64)

@@ -22,7 +22,6 @@ W_CHUNKS = D_IN // P
 BANK = 512
 PSUM_BANKS = 8
 WARM_FIRST = 4
-WARM_EVERY = 2
 WARM_EACH = 2
 
 FLOPS = 2 * 2 * ITEMS * HOPS * D_OUT * D_IN
@@ -76,7 +75,6 @@ def tile_dogtaitujuanji_pa_kernel(tc, x, w1a, w2a, grad_out, out):
     ):
         identity = const.tile([P, P], F32)
         make_identity(nc, identity[:])
-
         zeros = const.tile([P, BANK], BF16)
         nc.vector.memset(zeros[:], 0.0)
 
@@ -85,90 +83,133 @@ def tile_dogtaitujuanji_pa_kernel(tc, x, w1a, w2a, grad_out, out):
             for repeat in range(count):
                 nc.tensor.matmul(out=bank[:], lhsT=zeros[:, :P], rhs=zeros[:], start=True, stop=True)
 
-        groups_seen = []
-
-        def keep_warm_after_group():
-            groups_seen.append(1)
-            if len(groups_seen) % WARM_EVERY == 0:
-                keep_warm(WARM_EACH)
-
-        keep_warm(WARM_FIRST)
-
-        w_raw = []
-        for w in (w1a, w2a):
+        def load_weight(w):
+            pieces = []
             for chunk in range(W_CHUNKS):
                 w_piece = w_rows.tile([P, D_OUT], BF16)
                 nc.sync.dma_start(out=w_piece[:], in_=w[chunk * P : (chunk + 1) * P, :])
-                w_raw.append(w_piece)
-        g_raw = []
-        for block in range(BLOCKS):
+                pieces.append(w_piece)
+            return pieces
+
+        def load_block(block):
+            pieces = []
             for hop in range(HOPS):
                 g_piece = g_rows.tile([P, D_OUT], BF16)
                 nc.sync.dma_start(out=g_piece[:], in_=grad_out[block * P : (block + 1) * P, hop, :])
-                g_raw.append(g_piece)
+                pieces.append(g_piece)
+            return pieces
 
-        def quantise_weight(pieces):
+        w1_raw = load_weight(w1a)
+        w2_raw = load_weight(w2a)
+        g_raw = []
+        for block in range(BLOCKS):
+            g_raw.append(load_block(block))
+
+        def weight_tiles():
             w_grouped = w_keep.tile([P, PASSES * D_IN * PACK], BF16, align_bytes=64)
-            for chunk in range(W_CHUNKS):
-                bank = transpose_rows(nc, banks, identity, pieces[chunk][:])
-                keep_warm_after_group()
-                nc.vector.tensor_copy(
-                    out=as_words(w_grouped)[:, :, chunk * P : (chunk + 1) * P, :],
-                    in_=words_side_by_side(bank),
-                )
             w_codes = w_keep.tile([P, PASSES * D_IN], U32, align_bytes=64)
             w_scales = w_keep.tile([P, PASSES * D_IN], U8, align_bytes=64)
+            return w_grouped, w_codes, w_scales
+
+        w1_tiles = weight_tiles()
+        w2_tiles = weight_tiles()
+
+        def transpose_weight(tiles, pieces, chunk, on_vector):
+            bank = transpose_rows(nc, banks, identity, pieces[chunk][:])
+            grouped_words = as_words(tiles[0])[:, :, chunk * P : (chunk + 1) * P, :]
+            if on_vector:
+                nc.vector.tensor_copy(out=grouped_words, in_=words_side_by_side(bank))
+            else:
+                nc.scalar.copy(out=grouped_words, in_=words_side_by_side(bank))
+
+        def quantise_weight(tiles, chunk):
+            w_grouped, w_codes, w_scales = tiles
+            for g in range(PASSES):
+                first = g * D_IN + chunk * P
+                nc.vector.quantize_mx(
+                    out=w_codes[:, first : first + P].bitcast(E4M3_X4),
+                    scales=w_scales[:, first : first + P],
+                    in_=w_grouped[:, first * PACK : (first + P) * PACK],
+                )
+
+        def quantise_whole_weight(tiles):
+            w_grouped, w_codes, w_scales = tiles
             nc.vector.quantize_mx(out=w_codes[:].bitcast(E4M3_X4), scales=w_scales[:], in_=w_grouped[:])
-            return w_codes, w_scales
 
-        w1_codes, w1_scales = quantise_weight(w_raw[:W_CHUNKS])
-        w2_codes, w2_scales = quantise_weight(w_raw[W_CHUNKS:])
+        codes = {}
 
-        def quantise_block(block):
-            quantised = []
-            for hop in range(HOPS):
-                bank = transpose_rows(nc, banks, identity, g_raw[block * HOPS + hop][:])
-                if block < 2:
-                    keep_warm_after_group()
-                g_grouped = stage.tile([P, PASSES * P * PACK], BF16, align_bytes=64)
-                nc.scalar.copy(out=as_words(g_grouped), in_=words_side_by_side(bank))
-                g_codes = stage.tile([P, PASSES * P], U32, align_bytes=64)
-                g_scales = stage.tile([P, PASSES * P], U8, align_bytes=64)
-                nc.vector.quantize_mx(out=g_codes[:].bitcast(E5M2_X4), scales=g_scales[:], in_=g_grouped[:])
-                quantised.append((g_codes, g_scales))
-            return quantised
+        def quantise_hop(block, hop):
+            bank = transpose_rows(nc, banks, identity, g_raw[block][hop][:])
+            g_grouped = stage.tile([P, PASSES * P * PACK], BF16, align_bytes=64)
+            nc.scalar.copy(out=as_words(g_grouped), in_=words_side_by_side(bank))
+            g_codes = stage.tile([P, PASSES * P], U32, align_bytes=64)
+            g_scales = stage.tile([P, PASSES * P], U8, align_bytes=64)
+            nc.vector.quantize_mx(out=g_codes[:].bitcast(E5M2_X4), scales=g_scales[:], in_=g_grouped[:])
+            codes[(block, hop)] = (g_codes, g_scales)
 
-        def multiply_block(block, quantised):
-            b_bank_of_hop = []
-            b_copy_of_hop = []
-            for hop in range(HOPS):
-                g_codes, g_scales = quantised[hop]
-                b_bank = mx_product(nc, banks, g_codes, g_scales, w1_codes, w1_scales)
-                b_bank_of_hop.append(b_bank)
-                if hop < HOPS - 1:
-                    b_copy = stage.tile([P, D_IN], F32)
-                    nc.scalar.copy(out=b_copy[:], in_=b_bank[:])
-                    b_copy_of_hop.append(b_copy)
-            pair_for_hop = []
+        b_banks = {}
+        b_copies = {}
+        pairs = {}
+
+        def b_product(block, hop):
+            g_codes, g_scales = codes[(block, hop)]
+            b_bank = mx_product(nc, banks, g_codes, g_scales, w1_tiles[1], w1_tiles[2])
+            b_banks[(block, hop)] = b_bank
+            if hop < HOPS - 1:
+                b_copy = stage.tile([P, D_IN], F32)
+                nc.scalar.copy(out=b_copy[:], in_=b_bank[:])
+                b_copies[(block, hop)] = b_copy
+
+        def pair_sums(block):
             for hop in range(HOPS):
                 q, r = [other for other in range(HOPS) if other != hop]
                 pair = stage.tile([P, D_IN], F32)
                 if r == HOPS - 1:
-                    nc.vector.tensor_tensor(out=pair[:], in0=b_bank_of_hop[r][:], in1=b_copy_of_hop[q][:], op=ADD)
+                    nc.vector.tensor_tensor(out=pair[:], in0=b_banks[(block, r)][:], in1=b_copies[(block, q)][:], op=ADD)
                 else:
-                    nc.gpsimd.tensor_tensor(out=pair[:], in0=b_copy_of_hop[q][:], in1=b_copy_of_hop[r][:], op=ADD)
-                pair_for_hop.append(pair)
-            for hop in range(HOPS):
-                g_codes, g_scales = quantised[hop]
-                a_bank = mx_product(nc, banks, g_codes, g_scales, w2_codes, w2_scales)
-                result = stage.tile([P, D_IN], F32)
-                nc.vector.scalar_tensor_tensor(
-                    out=result[:], in0=pair_for_hop[hop][:], scalar=0.5, in1=a_bank[:], op0=MULT, op1=ADD
-                )
-                nc.sync.dma_start(out=out[block * P : (block + 1) * P, hop, :], in_=result[:])
+                    nc.gpsimd.tensor_tensor(out=pair[:], in0=b_copies[(block, q)][:], in1=b_copies[(block, r)][:], op=ADD)
+                pairs[(block, hop)] = pair
 
-        ready = quantise_block(0)
-        for block in range(BLOCKS):
-            following = quantise_block(block + 1) if block + 1 < BLOCKS else None
-            multiply_block(block, ready)
-            ready = following
+        def a_product(block, hop):
+            g_codes, g_scales = codes[(block, hop)]
+            a_bank = mx_product(nc, banks, g_codes, g_scales, w2_tiles[1], w2_tiles[2])
+            result = stage.tile([P, D_IN], F32)
+            nc.vector.scalar_tensor_tensor(
+                out=result[:], in0=pairs[(block, hop)][:], scalar=0.5, in1=a_bank[:], op0=MULT, op1=ADD
+            )
+            nc.sync.dma_start(out=out[block * P : (block + 1) * P, hop, :], in_=result[:])
+
+        def quantise_block(block):
+            for hop in range(HOPS):
+                quantise_hop(block, hop)
+
+        def b_products(block):
+            for hop in range(HOPS):
+                b_product(block, hop)
+            pair_sums(block)
+
+        def a_products(block):
+            for hop in range(HOPS):
+                a_product(block, hop)
+
+        keep_warm(WARM_FIRST)
+        for tiles, pieces in ((w1_tiles, w1_raw), (w2_tiles, w2_raw)):
+            for first_chunk in (0, 2):
+                transpose_weight(tiles, pieces, first_chunk, False)
+                transpose_weight(tiles, pieces, first_chunk + 1, True)
+                keep_warm(WARM_EACH)
+            if tiles is w1_tiles:
+                quantise_whole_weight(tiles)
+        quantise_hop(0, 0)
+        quantise_hop(0, 1)
+        keep_warm(WARM_EACH)
+        quantise_hop(0, 2)
+        quantise_whole_weight(w2_tiles)
+        b_products(0)
+        quantise_block(1)
+        a_products(0)
+        for block in range(1, BLOCKS):
+            if block + 1 < BLOCKS:
+                quantise_block(block + 1)
+            b_products(block)
+            a_products(block)

@@ -100,9 +100,9 @@ def tile_dogtaitujuanji_pa_kernel(tc, x, w1a, w2a, grad_out, out):
             return pieces
 
         w1_raw = load_weight(w1a)
+        g_raw = [load_block(0)]
         w2_raw = load_weight(w2a)
-        g_raw = []
-        for block in range(BLOCKS):
+        for block in range(1, BLOCKS):
             g_raw.append(load_block(block))
 
         def weight_tiles():
@@ -193,17 +193,21 @@ def tile_dogtaitujuanji_pa_kernel(tc, x, w1a, w2a, grad_out, out):
                 a_product(block, hop)
 
         keep_warm(WARM_FIRST)
-        for tiles, pieces in ((w1_tiles, w1_raw), (w2_tiles, w2_raw)):
-            for first_chunk in (0, 2):
-                transpose_weight(tiles, pieces, first_chunk, False)
-                transpose_weight(tiles, pieces, first_chunk + 1, True)
-                keep_warm(WARM_EACH)
-            if tiles is w1_tiles:
-                quantise_whole_weight(tiles)
+        for first_chunk in (0, 2):
+            transpose_weight(w1_tiles, w1_raw, first_chunk, False)
+            transpose_weight(w1_tiles, w1_raw, first_chunk + 1, True)
+            keep_warm(WARM_EACH)
+        quantise_whole_weight(w1_tiles)
         quantise_hop(0, 0)
         quantise_hop(0, 1)
         keep_warm(WARM_EACH)
         quantise_hop(0, 2)
+        transpose_weight(w2_tiles, w2_raw, 0, True)
+        keep_warm(WARM_EACH)
+        transpose_weight(w2_tiles, w2_raw, 1, False)
+        transpose_weight(w2_tiles, w2_raw, 2, True)
+        keep_warm(WARM_EACH)
+        transpose_weight(w2_tiles, w2_raw, 3, False)
         quantise_whole_weight(w2_tiles)
         b_products(0)
         quantise_block(1)

import concourse.mybir as mybir
from concourse.masks import make_identity

F32 = mybir.dt.float32
BF16 = mybir.dt.bfloat16
U32 = mybir.dt.uint32
U8 = mybir.dt.uint8
E4M3_X4 = mybir.dt.float8_e4m3fn_x4
E5M2_X4 = mybir.dt.float8_e5m2_x4
ADD = mybir.AluOpType.add
MULT = mybir.AluOpType.mult

ITEMS, HOPS, D_IN, D_OUT = 1024, 3, 512, 1024

P = 128
PACK = 4
HALVES = 2
K_PASS = P * PACK
PASSES = D_OUT // K_PASS
BLOCKS = ITEMS // P
W_CHUNKS = D_IN // P
BANK = 512
PSUM_BANKS = 8
WARM_FIRST = 4
WARM_EACH = 2

FLOPS = 2 * 2 * ITEMS * HOPS * D_OUT * D_IN
BYTES = 2 * ITEMS * HOPS * D_OUT + 2 * 2 * D_IN * D_OUT + 4 * ITEMS * HOPS * D_IN


def transpose_rows(nc, banks, identity, rows):
    words = rows.bitcast(F32)
    bank = banks.tile([P, BANK], F32, name="bank", tag="bank")
    for j in range(PASSES * HALVES):
        cols = slice(j * P, (j + 1) * P)
        nc.tensor.transpose(bank[:, cols], words[:, cols], identity[:])
    return bank


def words_side_by_side(bank):
    return bank[:].rearrange("p (g u c) -> p g c u", g=PASSES, u=HALVES)


def as_words(grouped):
    return grouped[:].bitcast(F32).rearrange("p (g c u) -> p g c u", g=PASSES, u=HALVES)


def mx_product(nc, banks, g_codes, g_scales, w_codes, w_scales):
    bank = banks.tile([P, BANK], F32, name="bank", tag="bank")
    for g in range(PASSES):
        items = slice(g * P, (g + 1) * P)
        features = slice(g * D_IN, (g + 1) * D_IN)
        nc.tensor.matmul_mx(
            out=bank[:],
            lhsT=g_codes[:, items].bitcast(E5M2_X4),
            lhsT_scale=g_scales[:, items],
            rhs=w_codes[:, features].bitcast(E4M3_X4),
            rhs_scale=w_scales[:, features],
            start=(g == 0),
            stop=(g == PASSES - 1),
        )
    return bank


def tile_dogtaitujuanji_pa_kernel(tc, x, w1a, w2a, grad_out, out):
    nc = tc.nc
    with (
        tc.manual_schedule(),
        tc.tile_pool(name="const", bufs=1) as const,
        tc.tile_pool(name="w_rows", bufs=2 * W_CHUNKS) as w_rows,
        tc.tile_pool(name="g_rows", bufs=BLOCKS * HOPS) as g_rows,
        tc.tile_pool(name="w_keep", bufs=2) as w_keep,
        tc.tile_pool(name="stage", bufs=3 * HOPS) as stage,
        tc.psum_pool(name="banks", bufs=PSUM_BANKS) as banks,
    ):
        identity = const.tile([P, P], F32)
        make_identity(nc, identity[:])
        zeros = const.tile([P, BANK], BF16)
        nc.vector.memset(zeros[:], 0.0)

        def keep_warm(count):
            bank = banks.tile([P, BANK], F32, name="bank", tag="bank")
            for repeat in range(count):
                nc.tensor.matmul(out=bank[:], lhsT=zeros[:, :P], rhs=zeros[:], start=True, stop=True)

        def load_weight(w):
            pieces = []
            for chunk in range(W_CHUNKS):
                w_piece = w_rows.tile([P, D_OUT], BF16)
                nc.sync.dma_start(out=w_piece[:], in_=w[chunk * P : (chunk + 1) * P, :])
                pieces.append(w_piece)
            return pieces

        def load_block(block):
            pieces = []
            for hop in range(HOPS):
                g_piece = g_rows.tile([P, D_OUT], BF16)
                nc.sync.dma_start(out=g_piece[:], in_=grad_out[block * P : (block + 1) * P, hop, :])
                pieces.append(g_piece)
            return pieces

        w1_raw = load_weight(w1a)
        g_raw = [load_block(0)]
        w2_raw = load_weight(w2a)
        for block in range(1, BLOCKS):
            g_raw.append(load_block(block))

        def weight_tiles():
            w_grouped = w_keep.tile([P, PASSES * D_IN * PACK], BF16, align_bytes=64)
            w_codes = w_keep.tile([P, PASSES * D_IN], U32, align_bytes=64)
            w_scales = w_keep.tile([P, PASSES * D_IN], U8, align_bytes=64)
            return w_grouped, w_codes, w_scales

        w1_tiles = weight_tiles()
        w2_tiles = weight_tiles()

        def transpose_weight(tiles, pieces, chunk, on_vector):
            bank = transpose_rows(nc, banks, identity, pieces[chunk][:])
            grouped_words = as_words(tiles[0])[:, :, chunk * P : (chunk + 1) * P, :]
            if on_vector:
                nc.vector.tensor_copy(out=grouped_words, in_=words_side_by_side(bank))
            else:
                nc.scalar.copy(out=grouped_words, in_=words_side_by_side(bank))

        def quantise_weight(tiles, chunk):
            w_grouped, w_codes, w_scales = tiles
            for g in range(PASSES):
                first = g * D_IN + chunk * P
                nc.vector.quantize_mx(
                    out=w_codes[:, first : first + P].bitcast(E4M3_X4),
                    scales=w_scales[:, first : first + P],
                    in_=w_grouped[:, first * PACK : (first + P) * PACK],
                )

        def quantise_whole_weight(tiles):
            w_grouped, w_codes, w_scales = tiles
            nc.vector.quantize_mx(out=w_codes[:].bitcast(E4M3_X4), scales=w_scales[:], in_=w_grouped[:])

        codes = {}

        def quantise_hop(block, hop):
            bank = transpose_rows(nc, banks, identity, g_raw[block][hop][:])
            g_grouped = stage.tile([P, PASSES * P * PACK], BF16, align_bytes=64)
            nc.scalar.copy(out=as_words(g_grouped), in_=words_side_by_side(bank))
            g_codes = stage.tile([P, PASSES * P], U32, align_bytes=64)
            g_scales = stage.tile([P, PASSES * P], U8, align_bytes=64)
            nc.vector.quantize_mx(out=g_codes[:].bitcast(E5M2_X4), scales=g_scales[:], in_=g_grouped[:])
            codes[(block, hop)] = (g_codes, g_scales)

        b_banks = {}
        b_copies = {}
        pairs = {}

        def b_product(block, hop):
            g_codes, g_scales = codes[(block, hop)]
            b_bank = mx_product(nc, banks, g_codes, g_scales, w1_tiles[1], w1_tiles[2])
            b_banks[(block, hop)] = b_bank
            if hop < HOPS - 1:
                b_copy = stage.tile([P, D_IN], F32)
                nc.scalar.copy(out=b_copy[:], in_=b_bank[:])
                b_copies[(block, hop)] = b_copy

        def pair_sums(block):
            for hop in range(HOPS):
                q, r = [other for other in range(HOPS) if other != hop]
                pair = stage.tile([P, D_IN], F32)
                if r == HOPS - 1:
                    nc.vector.tensor_tensor(out=pair[:], in0=b_banks[(block, r)][:], in1=b_copies[(block, q)][:], op=ADD)
                else:
                    nc.gpsimd.tensor_tensor(out=pair[:], in0=b_copies[(block, q)][:], in1=b_copies[(block, r)][:], op=ADD)
                pairs[(block, hop)] = pair

        def a_product(block, hop):
            g_codes, g_scales = codes[(block, hop)]
            a_bank = mx_product(nc, banks, g_codes, g_scales, w2_tiles[1], w2_tiles[2])
            result = stage.tile([P, D_IN], F32)
            nc.vector.scalar_tensor_tensor(
                out=result[:], in0=pairs[(block, hop)][:], scalar=0.5, in1=a_bank[:], op0=MULT, op1=ADD
            )
            nc.sync.dma_start(out=out[block * P : (block + 1) * P, hop, :], in_=result[:])

        def quantise_block(block):
            for hop in range(HOPS):
                quantise_hop(block, hop)

        def b_products(block):
            for hop in range(HOPS):
                b_product(block, hop)
            pair_sums(block)

        def a_products(block):
            for hop in range(HOPS):
                a_product(block, hop)

        keep_warm(WARM_FIRST)
        for first_chunk in (0, 2):
            transpose_weight(w1_tiles, w1_raw, first_chunk, False)
            transpose_weight(w1_tiles, w1_raw, first_chunk + 1, True)
            keep_warm(WARM_EACH)
        quantise_whole_weight(w1_tiles)
        quantise_hop(0, 0)
        quantise_hop(0, 1)
        keep_warm(WARM_EACH)
        quantise_hop(0, 2)
        transpose_weight(w2_tiles, w2_raw, 0, True)
        keep_warm(WARM_EACH)
        transpose_weight(w2_tiles, w2_raw, 1, False)
        transpose_weight(w2_tiles, w2_raw, 2, True)
        keep_warm(WARM_EACH)
        transpose_weight(w2_tiles, w2_raw, 3, False)
        quantise_whole_weight(w2_tiles)
        b_products(0)
        quantise_block(1)
        a_products(0)
        for block in range(1, BLOCKS):
            if block + 1 < BLOCKS:
                quantise_block(block + 1)
            b_products(block)
            a_products(block)
